import numpy as np
import ml_dtypes


def mxq(x, axis, fmt="e4m3"):
    dtype, down = {"e4m3": (ml_dtypes.float8_e4m3fn, 7), "e5m2": (ml_dtypes.float8_e5m2, 14)}[fmt]
    v = np.moveaxis(np.asarray(x, np.float32).astype(ml_dtypes.bfloat16).astype(np.float64), axis, -1)
    blocks = v.reshape(v.shape[:-1] + (-1, 32))
    amax = np.abs(blocks).max(-1, keepdims=True)
    byte = np.maximum(np.where(amax > 0, np.frexp(amax)[1] - 1 + 127, 0) - down, 1)
    scale = np.exp2(byte - 127.0)
    codes = (blocks / scale).astype(np.float32).astype(dtype).astype(np.float64)
    return np.moveaxis((codes * scale).reshape(v.shape), -1, axis)


WIDE = False


def mx_kscale(k):
    if not WIDE:
        return np.ones(k)
    levels = np.array([10, -10, 5, -5, 0])
    a = np.random.permutation(np.resize(levels, k // 512 * 4)).reshape(k // 512, 4)
    idx = np.arange(k)
    return np.exp2(a[idx // 512, idx % 128 // 32])


BF16 = ml_dtypes.bfloat16


def bf(x):
    return np.asarray(x, np.float32).astype(BF16)


def f64(x):
    return np.asarray(x).astype(np.float64)


B, H, S, D, P = 2, 4, 512, 256, 3


def setup_inputs():
    s = mx_kscale(S)
    g = np.exp2(np.round(np.log2(np.mean(s))))
    sign = np.where(np.random.standard_normal((H, 1)) < 0.0, -1.0, 1.0)
    q = np.random.standard_normal((B, H, S, D)) * 1.5
    k = np.random.standard_normal((B, H, S, D))
    v = np.random.standard_normal((B, H, S, D)) * 2.0
    q[..., 0] = 1.0
    k[..., 0] += np.log(s) * np.sqrt(D)
    v = v / s[:, None] * g
    return {
        "q": bf(q),
        "k": bf(k),
        "v": bf(v),
        "qs_s": bf(np.random.uniform(0.0, 1.0, (B, S, P))),
        "ks_s": bf(np.random.uniform(0.0, 1.0, (B, S, P))),
        "alpha": bf(sign * (1.5 + np.random.uniform(0.0, 1.0, (H, 1)))),
        "beta": bf(1.5 + 0.5 * np.random.standard_normal((H, 1))),
    }


def reference(q, k, v, qs_s, ks_s, alpha, beta):
    scale = 1.0 / np.sqrt(D)
    scores = (f64(q) @ f64(k).transpose(0, 1, 3, 2)) * scale
    d_sq = np.sum(np.square(f64(qs_s)[:, :, None, :] - f64(ks_s)[:, None, :, :]), axis=-1)
    a = f64(alpha)[:, 0][None, :, None, None]
    bexp = f64(beta)[:, 0][None, :, None, None]
    bias = a * np.exp(-bexp * d_sq[:, None, :, :])
    z = scores + bias
    e = np.exp(z - z.max(-1, keepdims=True))
    return (mxq(e, 3, "e4m3") @ mxq(f64(v), 2, "e4m3")) / e.sum(-1, keepdims=True)

@@ -1,0 +1,202 @@
+import math
+from contextlib import ExitStack
+
+import concourse.mybir as mybir
+from concourse.masks import make_identity
+
+F32 = mybir.dt.float32
+BF16 = mybir.dt.bfloat16
+U32 = mybir.dt.uint32
+U8 = mybir.dt.uint8
+FP8X4 = mybir.dt.float8_e4m3fn_x4
+ALU = mybir.AluOpType
+FUNC = mybir.ActivationFunctionType
+AXIS = mybir.AxisListType
+
+B, H, S, D, F = 2, 4, 512, 256, 3
+P = 128
+TILES = S // P
+CHUNKS = D // P
+PACK = 4
+HALVES = 2
+PAIR = 2
+
+FLOPS = 2 * 2 * B * H * S * S * D
+
+
+def tile_rbfbias_t_kernel(tc, q, k, v, qs_s, ks_s, alpha, beta, out):
+    nc = tc.nc
+    with ExitStack() as ctx:
+        const = ctx.enter_context(tc.tile_pool(name="const", bufs=1))
+        raw = ctx.enter_context(tc.tile_pool(name="raw", bufs=1))
+        operand = ctx.enter_context(tc.tile_pool(name="operand", bufs=1))
+        work = ctx.enter_context(tc.tile_pool(name="work", bufs=2))
+        psum = ctx.enter_context(tc.psum_pool(name="psum", bufs=2))
+
+        q_pos = const.tile([P, B, TILES * F], BF16)
+        nc.sync.dma_start(out=q_pos[:], in_=qs_s.rearrange("b (p t) f -> p b (t f)", t=TILES))
+        k_pos = const.tile([P, B * TILES, F], BF16)
+        nc.sync.dma_start(out=k_pos[:], in_=ks_s.rearrange("b (t p) f -> p (b t) f", p=P))
+        alpha_bf = const.tile([P, H], BF16)
+        nc.sync.dma_start(out=alpha_bf[:], in_=alpha.rearrange("h o -> (h o)").partition_broadcast(P))
+        beta_bf = const.tile([P, H], BF16)
+        nc.sync.dma_start(out=beta_bf[:], in_=beta.rearrange("h o -> (h o)").partition_broadcast(P))
+
+        k_raw, q_raw, v_raw = {}, {}, {}
+        for b in range(B):
+            for h in range(H):
+                k_raw[b, h] = raw.tile([P, TILES, D], BF16, name="k_raw_%d_%d" % (b, h))
+                nc.sync.dma_start(out=k_raw[b, h][:], in_=k[b, h].rearrange("(t p) d -> p t d", p=P))
+                q_raw[b, h] = raw.tile([P, TILES, D], BF16, name="q_raw_%d_%d" % (b, h))
+                nc.sync.dma_start(out=q_raw[b, h][:], in_=q[b, h].rearrange("(p t) d -> p t d", t=TILES))
+            for h in range(H):
+                v_raw[b, h] = raw.tile([P, PACK, D], BF16, name="v_raw_%d_%d" % (b, h))
+                nc.sync.dma_start(
+                    out=v_raw[b, h][:].rearrange("p (u e) d -> p u (e d)", e=HALVES),
+                    in_=v[b, h].rearrange("(u p e) d -> p u (e d)", p=P, e=HALVES),
+                )
+
+        ident_bf = const.tile([P, P], BF16)
+        make_identity(nc, ident_bf[:])
+        ident_f32 = const.tile([P, P], F32)
+        make_identity(nc, ident_f32[:])
+        alpha_f32 = const.tile([P, H], F32)
+        nc.vector.tensor_copy(out=alpha_f32[:], in_=alpha_bf[:])
+        neg_beta = const.tile([P, H], F32)
+        nc.vector.tensor_scalar_mul(out=neg_beta[:], in0=beta_bf[:], scalar1=-1.0)
+
+        def features(pos, linear_factor, square_at, ones_at, label):
+            feat = const.tile([P, B * TILES, P], BF16, name="feat_" + label)
+            nc.vector.memset(feat[:], 0.0)
+            nc.vector.memset(feat[:, :, ones_at : ones_at + 2 * F], 1.0)
+            nc.vector.tensor_scalar_mul(out=feat[:, :, 0:F], in0=pos, scalar1=linear_factor)
+            square = const.tile([P, B * TILES, F], F32, name="square_" + label)
+            nc.vector.tensor_mul(out=square[:], in0=pos, in1=pos)
+            hi = feat[:, :, square_at : square_at + F]
+            nc.vector.tensor_copy(out=hi, in_=square[:])
+            nc.vector.tensor_sub(out=feat[:, :, square_at + F : square_at + 2 * F], in0=square[:], in1=hi)
+            feat_ps = psum.tile([P, B * TILES, P], BF16, tag="turn", name="feat_ps_" + label)
+            for bt in range(B * TILES):
+                nc.tensor.transpose(feat_ps[:, bt, :], feat[:, bt, :], ident_bf[:])
+            feat_t = const.tile([P, B, S], BF16, name="feat_t_" + label)
+            nc.vector.tensor_copy(out=feat_t[:].rearrange("f b (t p) -> f (b t) p", p=P), in_=feat_ps[:])
+            return feat_t
+
+        q_feat = features(q_pos[:].rearrange("p b (t f) -> p (b t) f", f=F), -2.0, F, 3 * F, "q")
+        k_feat = features(k_pos[:], 1.0, 3 * F, F, "k")
+
+        k_t, q_t, v_codes, v_scales = {}, {}, {}, {}
+
+        def prepare_head(b, h):
+            k_ps = psum.tile([P, CHUNKS, S], BF16, tag="turn")
+            for t in range(TILES):
+                for c in range(CHUNKS):
+                    nc.tensor.transpose(
+                        k_ps[:, c, t * P : (t + 1) * P], k_raw[b, h][:, t, c * P : (c + 1) * P], ident_bf[:]
+                    )
+            k_t[b, h] = operand.tile([P, CHUNKS, S], BF16, name="k_t_%d_%d" % (b, h))
+            nc.scalar.copy(out=k_t[b, h][:], in_=k_ps[:])
+
+            q_ps = psum.tile([P, CHUNKS, S], BF16, tag="turn")
+            for t in range(TILES):
+                for c in range(CHUNKS):
+                    nc.tensor.transpose(
+                        q_ps[:, c, t * P : (t + 1) * P], q_raw[b, h][:, t, c * P : (c + 1) * P], ident_bf[:]
+                    )
+            q_t[b, h] = operand.tile([P, CHUNKS, S], BF16, name="q_t_%d_%d" % (b, h))
+            nc.vector.tensor_scalar_mul(out=q_t[b, h][:], in0=q_ps[:], scalar1=1.0 / math.sqrt(D))
+
+            v_grouped = work.tile([P, D, PACK], BF16, align_bytes=64)
+            nc.vector.tensor_copy(
+                out=v_grouped[:].rearrange("p (c i) r -> p c r i", i=4),
+                in_=v_raw[b, h][:].rearrange("p r (c i) -> p c r i", i=4),
+            )
+            v_codes[b, h] = operand.tile([P, D], U32, name="v_codes_%d_%d" % (b, h), align_bytes=64)
+            v_scales[b, h] = operand.tile([P, D], U8, name="v_scales_%d_%d" % (b, h), align_bytes=64)
+            nc.vector.quantize_mx(
+                out=v_codes[b, h][:].bitcast(FP8X4),
+                scales=v_scales[b, h][:],
+                in_=v_grouped[:].rearrange("p d r -> p (d r)"),
+            )
+
+        def attend(b, t):
+            queries = slice(t * P, (t + 1) * P)
+            d_sq = psum.tile([P, S], F32, tag="d_sq", bufs=1)
+            nc.tensor.matmul(d_sq[:], lhsT=q_feat[:, b, queries], rhs=k_feat[:, b, :], start=True, stop=True)
+
+            e_bf = work.tile([P, H * S], BF16)
+            neg_max = work.tile([P, H], F32)
+            row_sum = work.tile([P, H], F32)
+            for h in range(H):
+                scores = psum.tile([P, S], F32, tag="scores", bufs=3)
+                for c in range(CHUNKS):
+                    nc.tensor.matmul(
+                        scores[:],
+                        lhsT=q_t[b, h][:, c, queries],
+                        rhs=k_t[b, h][:, c, :],
+                        start=(c == 0),
+                        stop=(c == CHUNKS - 1),
+                    )
+                rbf = work.tile([P, S], F32, bufs=3)
+                nc.scalar.activation(out=rbf[:], in_=d_sq[:], func=FUNC.Exp, scale=neg_beta[:, h : h + 1])
+                z = work.tile([P, S], F32, bufs=4)
+                nc.vector.scalar_tensor_tensor(
+                    out=z[:], in0=rbf[:], scalar=alpha_f32[:, h : h + 1], in1=scores[:], op0=ALU.mult, op1=ALU.add
+                )
+                nc.vector.tensor_reduce(out=neg_max[:, h : h + 1], in_=z[:], axis=AXIS.X, op=ALU.max, negate=True)
+                nc.scalar.activation(
+                    out=e_bf[:, h * S : (h + 1) * S],
+                    in_=z[:],
+                    func=FUNC.Exp,
+                    bias=neg_max[:, h : h + 1],
+                    accum_out=row_sum[:, h : h + 1],
+                )
+
+            e_words = e_bf[:].bitcast(F32)
+            e_grouped = work.tile([P, H * P * PACK], BF16, align_bytes=64)
+            e_grouped_words = e_grouped[:].bitcast(F32).rearrange("p (h i u) -> p h i u", h=H, u=HALVES)
+            for pair in range(H // PAIR):
+                e_ps = psum.tile([P, PAIR, HALVES, P], F32, tag="turn")
+                for hh in range(PAIR):
+                    for u in range(HALVES):
+                        first = ((pair * PAIR + hh) * HALVES + u) * P
+                        nc.tensor.transpose(e_ps[:, hh, u, :], e_words[:, first : first + P], ident_f32[:])
+                copy_out = nc.scalar.copy if pair == 0 else nc.vector.tensor_copy
+                copy_out(
+                    out=e_grouped_words[:, pair * PAIR : (pair + 1) * PAIR],
+                    in_=e_ps[:].rearrange("p h u i -> p h i u"),
+                )
+            e_codes = work.tile([P, H * P], U32, align_bytes=64)
+            e_scales = work.tile([P, H * P], U8, align_bytes=64)
+            nc.vector.quantize_mx(out=e_codes[:].bitcast(FP8X4), scales=e_scales[:], in_=e_grouped[:])
+
+            inv_sum = work.tile([P, H], F32)
+            nc.vector.reciprocal(out=inv_sum[:], in_=row_sum[:])
+            result = work.tile([P, H, D], F32)
+            for pair in range(H // PAIR):
+                acc = psum.tile([P, PAIR, D], F32, tag="acc")
+                for hh in range(PAIR):
+                    h = pair * PAIR + hh
+                    nc.tensor.matmul_mx(
+                        out=acc[:, hh, :],
+                        lhsT=e_codes[:, h * P : (h + 1) * P].bitcast(FP8X4),
+                        lhsT_scale=e_scales[:, h * P : (h + 1) * P],
+                        rhs=v_codes[b, h][:].bitcast(FP8X4),
+                        rhs_scale=v_scales[b, h][:],
+                        start=True,
+                        stop=True,
+                    )
+                for hh in range(PAIR):
+                    h = pair * PAIR + hh
+                    nc.scalar.activation(
+                        out=result[:, h, :], in_=acc[:, hh, :], func=FUNC.Copy, scale=inv_sum[:, h : h + 1]
+                    )
+            nc.sync.dma_start(out=out[b].rearrange("h (p t) d -> t p h d", t=TILES)[t], in_=result[:])
+
+        for h in range(H):
+            prepare_head(0, h)
+        for t in range(TILES):
+            attend(0, t)
+            prepare_head(1, t)
+        for t in range(TILES):
+            attend(1, t)

@@ -20,13 +20,21 @@ CHUNKS = D // P
 PACK = 4
 HALVES = 2
 PAIR = 2
+GROUPS = B * TILES
+UNITS = GROUPS * H
 
 FLOPS = 2 * 2 * B * H * S * S * D
+
+
+def due(step, first, count):
+    n, rest = divmod(step - first, H)
+    return n if rest == 0 and 0 <= n < count else None
 
 
 def tile_rbfbias_t_kernel(tc, q, k, v, qs_s, ks_s, alpha, beta, out):
     nc = tc.nc
     with ExitStack() as ctx:
+        ctx.enter_context(tc.manual_schedule())
         const = ctx.enter_context(tc.tile_pool(name="const", bufs=1))
         raw = ctx.enter_context(tc.tile_pool(name="raw", bufs=1))
         operand = ctx.enter_context(tc.tile_pool(name="operand", bufs=1))
@@ -43,18 +51,35 @@ def tile_rbfbias_t_kernel(tc, q, k, v, qs_s, ks_s, alpha, beta, out):
         nc.sync.dma_start(out=beta_bf[:], in_=beta.rearrange("h o -> (h o)").partition_broadcast(P))
 
         k_raw, q_raw, v_raw = {}, {}, {}
-        for b in range(B):
-            for h in range(H):
-                k_raw[b, h] = raw.tile([P, TILES, D], BF16, name="k_raw_%d_%d" % (b, h))
-                nc.sync.dma_start(out=k_raw[b, h][:], in_=k[b, h].rearrange("(t p) d -> p t d", p=P))
-                q_raw[b, h] = raw.tile([P, TILES, D], BF16, name="q_raw_%d_%d" % (b, h))
-                nc.sync.dma_start(out=q_raw[b, h][:], in_=q[b, h].rearrange("(p t) d -> p t d", t=TILES))
-            for h in range(H):
-                v_raw[b, h] = raw.tile([P, PACK, D], BF16, name="v_raw_%d_%d" % (b, h))
-                nc.sync.dma_start(
-                    out=v_raw[b, h][:].rearrange("p (u e) d -> p u (e d)", e=HALVES),
-                    in_=v[b, h].rearrange("(u p e) d -> p u (e d)", p=P, e=HALVES),
-                )
+
+        def load_q(g):
+            b, t = divmod(g, TILES)
+            q_raw[g] = raw.tile([P, H, D], BF16, name="q_raw_%d" % g)
+            nc.sync.dma_start(out=q_raw[g][:], in_=q[b].rearrange("h (p t) d -> t p h d", t=TILES)[t])
+
+        def load_k(b, h):
+            k_raw[b, h] = raw.tile([P, TILES, D], BF16, name="k_raw_%d_%d" % (b, h))
+            nc.sync.dma_start(out=k_raw[b, h][:], in_=k[b, h].rearrange("(t p) d -> p t d", p=P))
+
+        def load_v(b, h):
+            v_raw[b, h] = raw.tile([P, PACK, D], BF16, name="v_raw_%d_%d" % (b, h))
+            nc.sync.dma_start(
+                out=v_raw[b, h][:].rearrange("p (u e) d -> p u (e d)", e=HALVES),
+                in_=v[b, h].rearrange("(u p e) d -> p u (e d)", p=P, e=HALVES),
+            )
+
+        load_q(0)
+        for h in range(H):
+            load_k(0, h)
+        load_q(1)
+        for h in range(H):
+            load_v(0, h)
+        for h in range(H):
+            load_k(1, h)
+            load_q(2 + h)
+            load_v(1, h)
+        for g in range(2 + H, GROUPS):
+            load_q(g)
 
         ident_bf = const.tile([P, P], BF16)
         make_identity(nc, ident_bf[:])
@@ -85,118 +110,217 @@ def tile_rbfbias_t_kernel(tc, q, k, v, qs_s, ks_s, alpha, beta, out):
         q_feat = features(q_pos[:].rearrange("p b (t f) -> p (b t) f", f=F), -2.0, F, 3 * F, "q")
         k_feat = features(k_pos[:], 1.0, 3 * F, F, "k")
 
-        k_t, q_t, v_codes, v_scales = {}, {}, {}, {}
+        k_ps, k_t, q_ps, q_t, v_grouped, v_codes, v_scales = {}, {}, {}, {}, {}, {}, {}
+        d_sq, scores, rbf, z, neg_max, row_sum, inv_sum, e_bf = {}, {}, {}, {}, {}, {}, {}, {}
+        e_ps, e_grouped, e_codes, e_scales, acc = {}, {}, {}, {}, {}
 
-        def prepare_head(b, h):
-            k_ps = psum.tile([P, CHUNKS, S], BF16, tag="turn")
+        def turn_k(b, h):
+            k_ps[b, h] = psum.tile([P, CHUNKS, S], BF16, tag="turn", name="k_ps")
             for t in range(TILES):
                 for c in range(CHUNKS):
                     nc.tensor.transpose(
-                        k_ps[:, c, t * P : (t + 1) * P], k_raw[b, h][:, t, c * P : (c + 1) * P], ident_bf[:]
+                        k_ps[b, h][:, c, t * P : (t + 1) * P], k_raw[b, h][:, t, c * P : (c + 1) * P], ident_bf[:]
                     )
+
+        def copy_k(b, h):
             k_t[b, h] = operand.tile([P, CHUNKS, S], BF16, name="k_t_%d_%d" % (b, h))
-            nc.scalar.copy(out=k_t[b, h][:], in_=k_ps[:])
+            nc.scalar.copy(out=k_t[b, h][:], in_=k_ps[b, h][:])
 
-            q_ps = psum.tile([P, CHUNKS, S], BF16, tag="turn")
-            for t in range(TILES):
+        def turn_q(g):
+            q_ps[g] = psum.tile([P, H, CHUNKS, P], BF16, tag="turn", name="q_ps")
+            for h in range(H):
                 for c in range(CHUNKS):
-                    nc.tensor.transpose(
-                        q_ps[:, c, t * P : (t + 1) * P], q_raw[b, h][:, t, c * P : (c + 1) * P], ident_bf[:]
-                    )
-            q_t[b, h] = operand.tile([P, CHUNKS, S], BF16, name="q_t_%d_%d" % (b, h))
-            nc.vector.tensor_scalar_mul(out=q_t[b, h][:], in0=q_ps[:], scalar1=1.0 / math.sqrt(D))
+                    nc.tensor.transpose(q_ps[g][:, h, c, :], q_raw[g][:, h, c * P : (c + 1) * P], ident_bf[:])
 
-            v_grouped = work.tile([P, D, PACK], BF16, align_bytes=64)
+        def copy_q(g):
+            q_t[g] = work.tile([P, H, CHUNKS, P], BF16, name="q_t", bufs=3)
+            nc.vector.tensor_scalar_mul(out=q_t[g][:], in0=q_ps[g][:], scalar1=1.0 / math.sqrt(D))
+
+        def regroup_v(b, h):
+            v_grouped[b, h] = work.tile([P, D, PACK], BF16, name="v_grouped", align_bytes=64)
             nc.vector.tensor_copy(
-                out=v_grouped[:].rearrange("p (c i) r -> p c r i", i=4),
+                out=v_grouped[b, h][:].rearrange("p (c i) r -> p c r i", i=4),
                 in_=v_raw[b, h][:].rearrange("p r (c i) -> p c r i", i=4),
             )
+
+        def quantise_v(b, h):
             v_codes[b, h] = operand.tile([P, D], U32, name="v_codes_%d_%d" % (b, h), align_bytes=64)
             v_scales[b, h] = operand.tile([P, D], U8, name="v_scales_%d_%d" % (b, h), align_bytes=64)
             nc.vector.quantize_mx(
                 out=v_codes[b, h][:].bitcast(FP8X4),
                 scales=v_scales[b, h][:],
-                in_=v_grouped[:].rearrange("p d r -> p (d r)"),
+                in_=v_grouped[b, h][:].rearrange("p d r -> p (d r)"),
             )
 
-        def attend(b, t):
-            queries = slice(t * P, (t + 1) * P)
-            d_sq = psum.tile([P, S], F32, tag="d_sq", bufs=1)
-            nc.tensor.matmul(d_sq[:], lhsT=q_feat[:, b, queries], rhs=k_feat[:, b, :], start=True, stop=True)
+        def distances(g):
+            b, t = divmod(g, TILES)
+            d_sq[g] = psum.tile([P, S], F32, name="d_sq")
+            nc.tensor.matmul(
+                d_sq[g][:], lhsT=q_feat[:, b, t * P : (t + 1) * P], rhs=k_feat[:, b, :], start=True, stop=True
+            )
 
-            e_bf = work.tile([P, H * S], BF16)
-            neg_max = work.tile([P, H], F32)
-            row_sum = work.tile([P, H], F32)
-            for h in range(H):
-                scores = psum.tile([P, S], F32, tag="scores", bufs=3)
-                for c in range(CHUNKS):
-                    nc.tensor.matmul(
-                        scores[:],
-                        lhsT=q_t[b, h][:, c, queries],
-                        rhs=k_t[b, h][:, c, :],
-                        start=(c == 0),
-                        stop=(c == CHUNKS - 1),
-                    )
-                rbf = work.tile([P, S], F32, bufs=3)
-                nc.scalar.activation(out=rbf[:], in_=d_sq[:], func=FUNC.Exp, scale=neg_beta[:, h : h + 1])
-                z = work.tile([P, S], F32, bufs=4)
-                nc.vector.scalar_tensor_tensor(
-                    out=z[:], in0=rbf[:], scalar=alpha_f32[:, h : h + 1], in1=scores[:], op0=ALU.mult, op1=ALU.add
+        def radial(u):
+            g, h = divmod(u, H)
+            rbf[u] = work.tile([P, S], F32, name="rbf", bufs=4)
+            nc.scalar.activation(out=rbf[u][:], in_=d_sq[g][:], func=FUNC.Exp, scale=neg_beta[:, h : h + 1])
+
+        def first_matmul(u):
+            g, h = divmod(u, H)
+            scores[u] = psum.tile([P, S], F32, name="scores")
+            for c in range(CHUNKS):
+                nc.tensor.matmul(
+                    scores[u][:],
+                    lhsT=q_t[g][:, h, c, :],
+                    rhs=k_t[g // TILES, h][:, c, :],
+                    start=(c == 0),
+                    stop=(c == CHUNKS - 1),
                 )
-                nc.vector.tensor_reduce(out=neg_max[:, h : h + 1], in_=z[:], axis=AXIS.X, op=ALU.max, negate=True)
+
+        def logits(u):
+            h = u % H
+            z[u] = work.tile([P, S], F32, name="z", bufs=4)
+            nc.vector.scalar_tensor_tensor(
+                out=z[u][:], in0=rbf[u][:], scalar=alpha_f32[:, h : h + 1], in1=scores[u][:], op0=ALU.mult, op1=ALU.add
+            )
+
+        def row_max(u):
+            g, h = divmod(u, H)
+            if h == 0:
+                neg_max[g] = work.tile([P, H], F32, name="neg_max")
+            nc.vector.tensor_reduce(out=neg_max[g][:, h : h + 1], in_=z[u][:], axis=AXIS.X, op=ALU.max, negate=True)
+
+        def exponent(u):
+            g, h = divmod(u, H)
+            if h == 0:
+                e_bf[g] = work.tile([P, H * S], BF16, name="e_bf")
+                row_sum[g] = work.tile([P, H], F32, name="row_sum")
+            nc.scalar.activation(
+                out=e_bf[g][:, h * S : (h + 1) * S],
+                in_=z[u][:],
+                func=FUNC.Exp,
+                bias=neg_max[g][:, h : h + 1],
+                accum_out=row_sum[g][:, h : h + 1],
+            )
+
+        def turn_e(g, pair):
+            e_words = e_bf[g][:].bitcast(F32)
+            e_ps[g, pair] = psum.tile([P, PAIR, HALVES, P], F32, tag="turn", name="e_ps")
+            for hh in range(PAIR):
+                for u in range(HALVES):
+                    first = ((pair * PAIR + hh) * HALVES + u) * P
+                    nc.tensor.transpose(e_ps[g, pair][:, hh, u, :], e_words[:, first : first + P], ident_f32[:])
+
+        def copy_e(g, pair, copy):
+            e_grouped[g, pair] = work.tile([P, PAIR * P * PACK], BF16, name="e_grouped", align_bytes=64)
+            copy(
+                out=e_grouped[g, pair][:].bitcast(F32).rearrange("p (h i u) -> p h i u", h=PAIR, u=HALVES),
+                in_=e_ps[g, pair][:].rearrange("p h u i -> p h i u"),
+            )
+
+        def quantise_e(g, pair):
+            e_codes[g, pair] = work.tile([P, PAIR * P], U32, name="e_codes", align_bytes=64)
+            e_scales[g, pair] = work.tile([P, PAIR * P], U8, name="e_scales", align_bytes=64)
+            nc.vector.quantize_mx(
+                out=e_codes[g, pair][:].bitcast(FP8X4), scales=e_scales[g, pair][:], in_=e_grouped[g, pair][:]
+            )
+
+        def reciprocal(g):
+            inv_sum[g] = work.tile([P, H], F32, name="inv_sum")
+            nc.vector.reciprocal(out=inv_sum[g][:], in_=row_sum[g][:])
+
+        def second_matmul(g, pair):
+            acc[g, pair] = psum.tile([P, PAIR, D], F32, name="acc")
+            for hh in range(PAIR):
+                h = pair * PAIR + hh
+                nc.tensor.matmul_mx(
+                    out=acc[g, pair][:, hh, :],
+                    lhsT=e_codes[g, pair][:, hh * P : (hh + 1) * P].bitcast(FP8X4),
+                    lhsT_scale=e_scales[g, pair][:, hh * P : (hh + 1) * P],
+                    rhs=v_codes[g // TILES, h][:].bitcast(FP8X4),
+                    rhs_scale=v_scales[g // TILES, h][:],
+                    start=True,
+                    stop=True,
+                )
+
+        def normalise(g, pair):
+            b, t = divmod(g, TILES)
+            result = work.tile([P, PAIR, D], F32, bufs=3)
+            for hh in range(PAIR):
+                h = pair * PAIR + hh
                 nc.scalar.activation(
-                    out=e_bf[:, h * S : (h + 1) * S],
-                    in_=z[:],
-                    func=FUNC.Exp,
-                    bias=neg_max[:, h : h + 1],
-                    accum_out=row_sum[:, h : h + 1],
+                    out=result[:, hh, :], in_=acc[g, pair][:, hh, :], func=FUNC.Copy, scale=inv_sum[g][:, h : h + 1]
                 )
+            heads = slice(pair * PAIR, (pair + 1) * PAIR)
+            nc.sync.dma_start(out=out[b].rearrange("h (p t) d -> t p h d", t=TILES)[t, :, heads, :], in_=result[:])
 
-            e_words = e_bf[:].bitcast(F32)
-            e_grouped = work.tile([P, H * P * PACK], BF16, align_bytes=64)
-            e_grouped_words = e_grouped[:].bitcast(F32).rearrange("p (h i u) -> p h i u", h=H, u=HALVES)
+        def k_due(step):
+            if 0 <= step + 5 < H:
+                return (0, step + 5)
+            h = due(step, 0, H)
+            return None if h is None else (1, h)
+
+        def v_due(step):
+            if 0 <= step + 1 < H:
+                return (0, step + 1)
+            h = due(step, 6, H)
+            return None if h is None else (1, h)
+
+        for s in range(-6, UNITS + 5):
+            if 0 <= s + 3 < UNITS:
+                first_matmul(s + 3)
+            g = due(s, -5, GROUPS)
+            if g is not None:
+                distances(g)
             for pair in range(H // PAIR):
-                e_ps = psum.tile([P, PAIR, HALVES, P], F32, tag="turn")
-                for hh in range(PAIR):
-                    for u in range(HALVES):
-                        first = ((pair * PAIR + hh) * HALVES + u) * P
-                        nc.tensor.transpose(e_ps[:, hh, u, :], e_words[:, first : first + P], ident_f32[:])
-                copy_out = nc.scalar.copy if pair == 0 else nc.vector.tensor_copy
-                copy_out(
-                    out=e_grouped_words[:, pair * PAIR : (pair + 1) * PAIR],
-                    in_=e_ps[:].rearrange("p h u i -> p h i u"),
-                )
-            e_codes = work.tile([P, H * P], U32, align_bytes=64)
-            e_scales = work.tile([P, H * P], U8, align_bytes=64)
-            nc.vector.quantize_mx(out=e_codes[:].bitcast(FP8X4), scales=e_scales[:], in_=e_grouped[:])
-
-            inv_sum = work.tile([P, H], F32)
-            nc.vector.reciprocal(out=inv_sum[:], in_=row_sum[:])
-            result = work.tile([P, H, D], F32)
+                g = due(s, 2 + 2 * pair, GROUPS)
+                if g is not None:
+                    turn_e(g, pair)
+            head = k_due(s)
+            if head is not None:
+                turn_k(head[0], head[1])
+            g = due(s, -6, GROUPS)
+            if g is not None:
+                turn_q(g)
             for pair in range(H // PAIR):
-                acc = psum.tile([P, PAIR, D], F32, tag="acc")
-                for hh in range(PAIR):
-                    h = pair * PAIR + hh
-                    nc.tensor.matmul_mx(
-                        out=acc[:, hh, :],
-                        lhsT=e_codes[:, h * P : (h + 1) * P].bitcast(FP8X4),
-                        lhsT_scale=e_scales[:, h * P : (h + 1) * P],
-                        rhs=v_codes[b, h][:].bitcast(FP8X4),
-                        rhs_scale=v_scales[b, h][:],
-                        start=True,
-                        stop=True,
-                    )
-                for hh in range(PAIR):
-                    h = pair * PAIR + hh
-                    nc.scalar.activation(
-                        out=result[:, h, :], in_=acc[:, hh, :], func=FUNC.Copy, scale=inv_sum[:, h : h + 1]
-                    )
-            nc.sync.dma_start(out=out[b].rearrange("h (p t) d -> t p h d", t=TILES)[t], in_=result[:])
+                g = due(s, 5 + 2 * pair, GROUPS)
+                if g is not None:
+                    second_matmul(g, pair)
 
-        for h in range(H):
-            prepare_head(0, h)
-        for t in range(TILES):
-            attend(0, t)
-            prepare_head(1, t)
-        for t in range(TILES):
-            attend(1, t)
+            if 0 <= s + 4 < UNITS:
+                radial(s + 4)
+            if 0 <= s < UNITS:
+                exponent(s)
+            head = k_due(s - 1)
+            if head is not None:
+                copy_k(head[0], head[1])
+            g = due(s, 3, GROUPS)
+            if g is not None:
+                copy_e(g, 0, nc.scalar.copy)
+            for pair in range(H // PAIR):
+                g = due(s, 6 + 2 * pair, GROUPS)
+                if g is not None:
+                    normalise(g, pair)
+
+            if 0 <= s + 2 < UNITS:
+                logits(s + 2)
+            if 0 <= s + 1 < UNITS:
+                row_max(s + 1)
+            g = due(s, 4, GROUPS)
+            if g is not None:
+                reciprocal(g)
+            for pair in range(H // PAIR):
+                g = due(s, 4 + 2 * pair, GROUPS)
+                if g is not None:
+                    quantise_e(g, pair)
+            g = due(s, 5, GROUPS)
+            if g is not None:
+                copy_e(g, 1, nc.vector.tensor_copy)
+            g = due(s, -5, GROUPS)
+            if g is not None:
+                copy_q(g)
+            head = v_due(s - 2)
+            if head is not None:
+                quantise_v(head[0], head[1])
+            head = v_due(s)
+            if head is not None:
+                regroup_v(head[0], head[1])

@@ -22,6 +22,8 @@ HALVES = 2
 PAIR = 2
 GROUPS = B * TILES
 UNITS = GROUPS * H
+SIDES = 2
+POS_PAD = 32
 
 FLOPS = 2 * 2 * B * H * S * S * D
 
@@ -41,78 +43,107 @@ def tile_rbfbias_t_kernel(tc, q, k, v, qs_s, ks_s, alpha, beta, out):
         work = ctx.enter_context(tc.tile_pool(name="work", bufs=2))
         psum = ctx.enter_context(tc.psum_pool(name="psum", bufs=2))
 
-        q_pos = const.tile([P, B, TILES * F], BF16)
-        nc.sync.dma_start(out=q_pos[:], in_=qs_s.rearrange("b (p t) f -> p b (t f)", t=TILES))
-        k_pos = const.tile([P, B * TILES, F], BF16)
-        nc.sync.dma_start(out=k_pos[:], in_=ks_s.rearrange("b (t p) f -> p (b t) f", p=P))
-        alpha_bf = const.tile([P, H], BF16)
-        nc.sync.dma_start(out=alpha_bf[:], in_=alpha.rearrange("h o -> (h o)").partition_broadcast(P))
-        beta_bf = const.tile([P, H], BF16)
-        nc.sync.dma_start(out=beta_bf[:], in_=beta.rearrange("h o -> (h o)").partition_broadcast(P))
+        def k_due(step):
+            h, rest = divmod(step + 11, 2)
+            if rest == 0 and 0 <= h < H:
+                return (0, h)
+            h = due(step, 0, H)
+            return None if h is None else (1, h)
 
-        k_raw, q_raw, v_raw = {}, {}, {}
+        def v_due(step):
+            if 0 <= step + 3 < H:
+                return (0, step + 3)
+            h = due(step, 8, H)
+            return None if h is None else (1, h)
 
-        def load_q(g):
-            b, t = divmod(g, TILES)
-            q_raw[g] = raw.tile([P, H, D], BF16, name="q_raw_%d" % g)
-            nc.sync.dma_start(out=q_raw[g][:], in_=q[b].rearrange("h (p t) d -> t p h d", t=TILES)[t])
-
-        def load_k(b, h):
-            k_raw[b, h] = raw.tile([P, TILES, D], BF16, name="k_raw_%d_%d" % (b, h))
-            nc.sync.dma_start(out=k_raw[b, h][:], in_=k[b, h].rearrange("(t p) d -> p t d", p=P))
-
-        def load_v(b, h):
-            v_raw[b, h] = raw.tile([P, PACK, D], BF16, name="v_raw_%d_%d" % (b, h))
-            nc.sync.dma_start(
-                out=v_raw[b, h][:].rearrange("p (u e) d -> p u (e d)", e=HALVES),
-                in_=v[b, h].rearrange("(u p e) d -> p u (e d)", p=P, e=HALVES),
-            )
-
-        load_q(0)
-        for h in range(H):
-            load_k(0, h)
-        load_q(1)
-        for h in range(H):
-            load_v(0, h)
-        for h in range(H):
-            load_k(1, h)
-            load_q(2 + h)
-            load_v(1, h)
-        for g in range(2 + H, GROUPS):
-            load_q(g)
+        first_step, last_step = -12, UNITS + 8
 
         ident_bf = const.tile([P, P], BF16)
         make_identity(nc, ident_bf[:])
         ident_f32 = const.tile([P, P], F32)
         make_identity(nc, ident_f32[:])
+
+        pos = const.tile([P, SIDES, POS_PAD], BF16)
+        nc.scalar.dma_start(
+            out=pos[:, 0, 0 : B * TILES * F].rearrange("p (b x) -> p b x", b=B),
+            in_=qs_s.rearrange("b (p t) f -> p b (t f)", t=TILES),
+        )
+        nc.scalar.dma_start(
+            out=pos[:, 1, 0 : B * TILES * F].rearrange("p (x f) -> p x f", f=F),
+            in_=ks_s.rearrange("b (t p) f -> p (b t) f", p=P),
+        )
+        alpha_bf = const.tile([P, H], BF16)
+        nc.scalar.dma_start(out=alpha_bf[:], in_=alpha.rearrange("h o -> (h o)").partition_broadcast(P))
+        beta_bf = const.tile([P, H], BF16)
+        nc.scalar.dma_start(out=beta_bf[:], in_=beta.rearrange("h o -> (h o)").partition_broadcast(P))
+
+        k_raw, q_raw, v_raw, v_grouped = {}, {}, {}, {}
+        for s in range(first_step, last_step + 1):
+            head = k_due(s)
+            if head is not None:
+                k_raw[head] = raw.tile([P, TILES, D], BF16, name="k_raw_%d_%d" % head)
+                nc.sync.dma_start(out=k_raw[head][:], in_=k[head[0], head[1]].rearrange("(t p) d -> p t d", p=P))
+            g = due(s, -12, GROUPS)
+            if g is not None:
+                q_raw[g] = raw.tile([P, H, D], BF16, name="q_raw_%d" % g)
+                nc.sync.dma_start(
+                    out=q_raw[g][:], in_=q[g // TILES].rearrange("h (p t) d -> t p h d", t=TILES)[g % TILES]
+                )
+            head = v_due(s)
+            if head is not None:
+                v_raw[head] = raw.tile([P, PACK, D], BF16, name="v_raw_%d_%d" % head)
+                nc.sync.dma_start(
+                    out=v_raw[head][:].rearrange("p (u e) d -> p u (e d)", e=HALVES),
+                    in_=v[head[0], head[1]].rearrange("(u p e) d -> p u (e d)", p=P, e=HALVES),
+                )
+                v_grouped[head] = operand.tile([P, D, PACK], BF16, name="v_grouped_%d_%d" % head, align_bytes=64)
+                nc.gpsimd.tensor_scalar(
+                    out=v_grouped[head][:],
+                    in0=v_raw[head][:].rearrange("p r d -> p d r"),
+                    scalar1=1.0,
+                    scalar2=0.0,
+                    op0=ALU.mult,
+                    op1=ALU.add,
+                )
+
+        square_at = (F, 3 * F)
+        ones_at = (3 * F, F)
+        feat = const.tile([P, SIDES, B * TILES, P], BF16)
+        nc.vector.memset(feat[:], 0.0)
+        for side in range(SIDES):
+            nc.vector.memset(feat[:, side, :, ones_at[side] : ones_at[side] + 2 * F], 1.0)
+        x = pos[:, :, 0 : B * TILES * F]
+        half_square = const.tile([P, SIDES, B * TILES * F], F32)
+        nc.vector.scalar_tensor_tensor(out=half_square[:], in0=x, scalar=-0.5, in1=x, op0=ALU.mult, op1=ALU.mult)
+        nc.vector.tensor_copy(out=feat[:, :, :, 0:F], in_=x.rearrange("p s (x f) -> p s x f", f=F))
+        for part in range(2):
+            for side in range(SIDES):
+                exact = half_square[:, side, :].rearrange("p (x f) -> p x f", f=F)
+                hi = feat[:, side, :, square_at[side] : square_at[side] + F]
+                if part == 0:
+                    nc.vector.tensor_copy(out=hi, in_=exact)
+                else:
+                    lo = feat[:, side, :, square_at[side] + F : square_at[side] + 2 * F]
+                    nc.vector.tensor_sub(out=lo, in0=exact, in1=hi)
+        two_beta = const.tile([P, H], F32)
+        nc.vector.tensor_scalar_mul(out=two_beta[:], in0=beta_bf[:], scalar1=2.0)
         alpha_f32 = const.tile([P, H], F32)
         nc.vector.tensor_copy(out=alpha_f32[:], in_=alpha_bf[:])
-        neg_beta = const.tile([P, H], F32)
-        nc.vector.tensor_scalar_mul(out=neg_beta[:], in0=beta_bf[:], scalar1=-1.0)
 
-        def features(pos, linear_factor, square_at, ones_at, label):
-            feat = const.tile([P, B * TILES, P], BF16, name="feat_" + label)
-            nc.vector.memset(feat[:], 0.0)
-            nc.vector.memset(feat[:, :, ones_at : ones_at + 2 * F], 1.0)
-            nc.vector.tensor_scalar_mul(out=feat[:, :, 0:F], in0=pos, scalar1=linear_factor)
-            square = const.tile([P, B * TILES, F], F32, name="square_" + label)
-            nc.vector.tensor_mul(out=square[:], in0=pos, in1=pos)
-            hi = feat[:, :, square_at : square_at + F]
-            nc.vector.tensor_copy(out=hi, in_=square[:])
-            nc.vector.tensor_sub(out=feat[:, :, square_at + F : square_at + 2 * F], in0=square[:], in1=hi)
-            feat_ps = psum.tile([P, B * TILES, P], BF16, tag="turn", name="feat_ps_" + label)
-            for bt in range(B * TILES):
-                nc.tensor.transpose(feat_ps[:, bt, :], feat[:, bt, :], ident_bf[:])
-            feat_t = const.tile([P, B, S], BF16, name="feat_t_" + label)
-            nc.vector.tensor_copy(out=feat_t[:].rearrange("f b (t p) -> f (b t) p", p=P), in_=feat_ps[:])
-            return feat_t
-
-        q_feat = features(q_pos[:].rearrange("p b (t f) -> p (b t) f", f=F), -2.0, F, 3 * F, "q")
-        k_feat = features(k_pos[:], 1.0, 3 * F, F, "k")
-
-        k_ps, k_t, q_ps, q_t, v_grouped, v_codes, v_scales = {}, {}, {}, {}, {}, {}, {}
+        k_ps, k_t, q_ps, q_t, v_codes, v_scales = {}, {}, {}, {}, {}, {}
         d_sq, scores, rbf, z, neg_max, row_sum, inv_sum, e_bf = {}, {}, {}, {}, {}, {}, {}, {}
         e_ps, e_grouped, e_codes, e_scales, acc = {}, {}, {}, {}, {}
+        feat_ps, feat_t = {}, {}
+
+        def turn_features(b):
+            feat_ps[b] = psum.tile([P, SIDES, TILES, P], BF16, tag="acc", name="feat_ps")
+            for side in range(SIDES):
+                for t in range(TILES):
+                    nc.tensor.transpose(feat_ps[b][:, side, t, :], feat[:, side, b * TILES + t, :], ident_bf[:])
+
+        def copy_features(b):
+            feat_t[b] = const.tile([P, SIDES, S], BF16, name="feat_t_%d" % b)
+            nc.vector.tensor_copy(out=feat_t[b][:].rearrange("f s (t p) -> f s t p", p=P), in_=feat_ps[b][:])
 
         def turn_k(b, h):
             k_ps[b, h] = psum.tile([P, CHUNKS, S], BF16, tag="turn", name="k_ps")
@@ -133,15 +164,8 @@ def tile_rbfbias_t_kernel(tc, q, k, v, qs_s, ks_s, alpha, beta, out):
                     nc.tensor.transpose(q_ps[g][:, h, c, :], q_raw[g][:, h, c * P : (c + 1) * P], ident_bf[:])
 
         def copy_q(g):
-            q_t[g] = work.tile([P, H, CHUNKS, P], BF16, name="q_t", bufs=3)
+            q_t[g] = work.tile([P, H, CHUNKS, P], BF16, name="q_t", bufs=4)
             nc.vector.tensor_scalar_mul(out=q_t[g][:], in0=q_ps[g][:], scalar1=1.0 / math.sqrt(D))
-
-        def regroup_v(b, h):
-            v_grouped[b, h] = work.tile([P, D, PACK], BF16, name="v_grouped", align_bytes=64)
-            nc.vector.tensor_copy(
-                out=v_grouped[b, h][:].rearrange("p (c i) r -> p c r i", i=4),
-                in_=v_raw[b, h][:].rearrange("p r (c i) -> p c r i", i=4),
-            )
 
         def quantise_v(b, h):
             v_codes[b, h] = operand.tile([P, D], U32, name="v_codes_%d_%d" % (b, h), align_bytes=64)
@@ -156,13 +180,13 @@ def tile_rbfbias_t_kernel(tc, q, k, v, qs_s, ks_s, alpha, beta, out):
             b, t = divmod(g, TILES)
             d_sq[g] = psum.tile([P, S], F32, name="d_sq")
             nc.tensor.matmul(
-                d_sq[g][:], lhsT=q_feat[:, b, t * P : (t + 1) * P], rhs=k_feat[:, b, :], start=True, stop=True
+                d_sq[g][:], lhsT=feat_t[b][:, 0, t * P : (t + 1) * P], rhs=feat_t[b][:, 1, :], start=True, stop=True
             )
 
         def radial(u):
             g, h = divmod(u, H)
-            rbf[u] = work.tile([P, S], F32, name="rbf", bufs=4)
-            nc.scalar.activation(out=rbf[u][:], in_=d_sq[g][:], func=FUNC.Exp, scale=neg_beta[:, h : h + 1])
+            rbf[u] = work.tile([P, S], F32, name="rbf", bufs=6)
+            nc.scalar.activation(out=rbf[u][:], in_=d_sq[g][:], func=FUNC.Exp, scale=two_beta[:, h : h + 1])
 
         def first_matmul(u):
             g, h = divmod(u, H)
@@ -178,7 +202,7 @@ def tile_rbfbias_t_kernel(tc, q, k, v, qs_s, ks_s, alpha, beta, out):
 
         def logits(u):
             h = u % H
-            z[u] = work.tile([P, S], F32, name="z", bufs=4)
+            z[u] = work.tile([P, S], F32, name="z", bufs=8)
             nc.vector.scalar_tensor_tensor(
                 out=z[u][:], in0=rbf[u][:], scalar=alpha_f32[:, h : h + 1], in1=scores[u][:], op0=ALU.mult, op1=ALU.add
             )
@@ -186,14 +210,14 @@ def tile_rbfbias_t_kernel(tc, q, k, v, qs_s, ks_s, alpha, beta, out):
         def row_max(u):
             g, h = divmod(u, H)
             if h == 0:
-                neg_max[g] = work.tile([P, H], F32, name="neg_max")
+                neg_max[g] = work.tile([P, H], F32, name="neg_max", bufs=3)
             nc.vector.tensor_reduce(out=neg_max[g][:, h : h + 1], in_=z[u][:], axis=AXIS.X, op=ALU.max, negate=True)
 
         def exponent(u):
             g, h = divmod(u, H)
             if h == 0:
-                e_bf[g] = work.tile([P, H * S], BF16, name="e_bf")
-                row_sum[g] = work.tile([P, H], F32, name="row_sum")
+                e_bf[g] = work.tile([P, H * S], BF16, name="e_bf", bufs=3)
+                row_sum[g] = work.tile([P, H], F32, name="row_sum", bufs=3)
             nc.scalar.activation(
                 out=e_bf[g][:, h * S : (h + 1) * S],
                 in_=z[u][:],
@@ -211,21 +235,21 @@ def tile_rbfbias_t_kernel(tc, q, k, v, qs_s, ks_s, alpha, beta, out):
                     nc.tensor.transpose(e_ps[g, pair][:, hh, u, :], e_words[:, first : first + P], ident_f32[:])
 
         def copy_e(g, pair, copy):
-            e_grouped[g, pair] = work.tile([P, PAIR * P * PACK], BF16, name="e_grouped", align_bytes=64)
+            e_grouped[g, pair] = work.tile([P, PAIR * P * PACK], BF16, name="e_grouped", bufs=4, align_bytes=64)
             copy(
                 out=e_grouped[g, pair][:].bitcast(F32).rearrange("p (h i u) -> p h i u", h=PAIR, u=HALVES),
                 in_=e_ps[g, pair][:].rearrange("p h u i -> p h i u"),
             )
 
         def quantise_e(g, pair):
-            e_codes[g, pair] = work.tile([P, PAIR * P], U32, name="e_codes", align_bytes=64)
-            e_scales[g, pair] = work.tile([P, PAIR * P], U8, name="e_scales", align_bytes=64)
+            e_codes[g, pair] = work.tile([P, PAIR * P], U32, name="e_codes", bufs=3, align_bytes=64)
+            e_scales[g, pair] = work.tile([P, PAIR * P], U8, name="e_scales", bufs=3, align_bytes=64)
             nc.vector.quantize_mx(
                 out=e_codes[g, pair][:].bitcast(FP8X4), scales=e_scales[g, pair][:], in_=e_grouped[g, pair][:]
             )
 
         def reciprocal(g):
-            inv_sum[g] = work.tile([P, H], F32, name="inv_sum")
+            inv_sum[g] = work.tile([P, H], F32, name="inv_sum", bufs=3)
             nc.vector.reciprocal(out=inv_sum[g][:], in_=row_sum[g][:])
 
         def second_matmul(g, pair):
@@ -253,41 +277,32 @@ def tile_rbfbias_t_kernel(tc, q, k, v, qs_s, ks_s, alpha, beta, out):
             heads = slice(pair * PAIR, (pair + 1) * PAIR)
             nc.sync.dma_start(out=out[b].rearrange("h (p t) d -> t p h d", t=TILES)[t, :, heads, :], in_=result[:])
 
-        def k_due(step):
-            if 0 <= step + 5 < H:
-                return (0, step + 5)
-            h = due(step, 0, H)
-            return None if h is None else (1, h)
-
-        def v_due(step):
-            if 0 <= step + 1 < H:
-                return (0, step + 1)
-            h = due(step, 6, H)
-            return None if h is None else (1, h)
-
-        for s in range(-6, UNITS + 5):
-            if 0 <= s + 3 < UNITS:
-                first_matmul(s + 3)
-            g = due(s, -5, GROUPS)
-            if g is not None:
-                distances(g)
+        for s in range(first_step, last_step + 1):
+            if 0 <= s + 5 < UNITS:
+                first_matmul(s + 5)
             for pair in range(H // PAIR):
-                g = due(s, 2 + 2 * pair, GROUPS)
+                g = due(s, 2 + 4 * pair, GROUPS)
                 if g is not None:
                     turn_e(g, pair)
             head = k_due(s)
             if head is not None:
                 turn_k(head[0], head[1])
-            g = due(s, -6, GROUPS)
+            g = due(s, -12, GROUPS)
             if g is not None:
                 turn_q(g)
+            b = due(s, -10, GROUPS)
+            if b is not None and b % TILES == 0:
+                turn_features(b // TILES)
             for pair in range(H // PAIR):
-                g = due(s, 5 + 2 * pair, GROUPS)
+                g = due(s, 9 + 2 * pair, GROUPS)
                 if g is not None:
                     second_matmul(g, pair)
+            g = due(s, -8, GROUPS)
+            if g is not None:
+                distances(g)
 
-            if 0 <= s + 4 < UNITS:
-                radial(s + 4)
+            if 0 <= s + 7 < UNITS:
+                radial(s + 7)
             if 0 <= s < UNITS:
                 exponent(s)
             head = k_due(s - 1)
@@ -297,30 +312,30 @@ def tile_rbfbias_t_kernel(tc, q, k, v, qs_s, ks_s, alpha, beta, out):
             if g is not None:
                 copy_e(g, 0, nc.scalar.copy)
             for pair in range(H // PAIR):
-                g = due(s, 6 + 2 * pair, GROUPS)
+                g = due(s, 10 + 2 * pair, GROUPS)
                 if g is not None:
                     normalise(g, pair)
 
-            if 0 <= s + 2 < UNITS:
-                logits(s + 2)
-            if 0 <= s + 1 < UNITS:
-                row_max(s + 1)
-            g = due(s, 4, GROUPS)
+            if 0 <= s + 4 < UNITS:
+                logits(s + 4)
+            if 0 <= s + 3 < UNITS:
+                row_max(s + 3)
+            b = due(s, -9, GROUPS)
+            if b is not None and b % TILES == 0:
+                copy_features(b // TILES)
+            g = due(s, 6, GROUPS)
             if g is not None:
                 reciprocal(g)
             for pair in range(H // PAIR):
-                g = due(s, 4 + 2 * pair, GROUPS)
+                g = due(s, 6 + 2 * pair, GROUPS)
                 if g is not None:
                     quantise_e(g, pair)
-            g = due(s, 5, GROUPS)
+            g = due(s, 7, GROUPS)
             if g is not None:
                 copy_e(g, 1, nc.vector.tensor_copy)
-            g = due(s, -5, GROUPS)
+            g = due(s, -11, GROUPS)
             if g is not None:
                 copy_q(g)
-            head = v_due(s - 2)
+            head = v_due(s - 3)
             if head is not None:
                 quantise_v(head[0], head[1])
-            head = v_due(s)
-            if head is not None:
-                regroup_v(head[0], head[1])

@@ -56,7 +56,7 @@ def tile_rbfbias_t_kernel(tc, q, k, v, qs_s, ks_s, alpha, beta, out):
             h = due(step, 8, H)
             return None if h is None else (1, h)
 
-        first_step, last_step = -12, UNITS + 8
+        first_step, last_step = -12, UNITS + 6
 
         ident_bf = const.tile([P, P], BF16)
         make_identity(nc, ident_bf[:])
@@ -268,13 +268,20 @@ def tile_rbfbias_t_kernel(tc, q, k, v, qs_s, ks_s, alpha, beta, out):
 
         def normalise(g, pair):
             b, t = divmod(g, TILES)
-            result = work.tile([P, PAIR, D], F32, bufs=3)
-            for hh in range(PAIR):
-                h = pair * PAIR + hh
-                nc.scalar.activation(
-                    out=result[:, hh, :], in_=acc[g, pair][:, hh, :], func=FUNC.Copy, scale=inv_sum[g][:, h : h + 1]
-                )
             heads = slice(pair * PAIR, (pair + 1) * PAIR)
+            result = work.tile([P, PAIR, D], F32, bufs=4)
+            if pair == 0:
+                for hh in range(PAIR):
+                    nc.scalar.activation(
+                        out=result[:, hh, :], in_=acc[g, pair][:, hh, :], func=FUNC.Copy, scale=inv_sum[g][:, hh : hh + 1]
+                    )
+            else:
+                nc.vector.tensor_tensor(
+                    out=result[:],
+                    in0=acc[g, pair][:],
+                    in1=inv_sum[g][:, heads].unsqueeze(2).to_broadcast([P, PAIR, D]),
+                    op=ALU.mult,
+                )
             nc.sync.dma_start(out=out[b].rearrange("h (p t) d -> t p h d", t=TILES)[t, :, heads, :], in_=result[:])
 
         for s in range(first_step, last_step + 1):
@@ -294,7 +301,7 @@ def tile_rbfbias_t_kernel(tc, q, k, v, qs_s, ks_s, alpha, beta, out):
             if b is not None and b % TILES == 0:
                 turn_features(b // TILES)
             for pair in range(H // PAIR):
-                g = due(s, 9 + 2 * pair, GROUPS)
+                g = due(s, 9, GROUPS)
                 if g is not None:
                     second_matmul(g, pair)
             g = due(s, -8, GROUPS)
@@ -311,10 +318,9 @@ def tile_rbfbias_t_kernel(tc, q, k, v, qs_s, ks_s, alpha, beta, out):
             g = due(s, 3, GROUPS)
             if g is not None:
                 copy_e(g, 0, nc.scalar.copy)
-            for pair in range(H // PAIR):
-                g = due(s, 10 + 2 * pair, GROUPS)
-                if g is not None:
-                    normalise(g, pair)
+            g = due(s, 10, GROUPS)
+            if g is not None:
+                normalise(g, 0)
 
             if 0 <= s + 4 < UNITS:
                 logits(s + 4)
@@ -333,6 +339,9 @@ def tile_rbfbias_t_kernel(tc, q, k, v, qs_s, ks_s, alpha, beta, out):
             g = due(s, 7, GROUPS)
             if g is not None:
                 copy_e(g, 1, nc.vector.tensor_copy)
+            g = due(s, 10, GROUPS)
+            if g is not None:
+                normalise(g, 1)
             g = due(s, -11, GROUPS)
             if g is not None:
                 copy_q(g)

import math
from contextlib import ExitStack

import concourse.mybir as mybir
from concourse.masks import make_identity

F32 = mybir.dt.float32
BF16 = mybir.dt.bfloat16
U32 = mybir.dt.uint32
U8 = mybir.dt.uint8
FP8X4 = mybir.dt.float8_e4m3fn_x4
ALU = mybir.AluOpType
FUNC = mybir.ActivationFunctionType
AXIS = mybir.AxisListType

B, H, S, D, F = 2, 4, 512, 256, 3
P = 128
TILES = S // P
CHUNKS = D // P
PACK = 4
HALVES = 2
PAIR = 2
GROUPS = B * TILES
UNITS = GROUPS * H
SIDES = 2
POS_PAD = 32

FLOPS = 2 * 2 * B * H * S * S * D


def due(step, first, count):
    n, rest = divmod(step - first, H)
    return n if rest == 0 and 0 <= n < count else None


def tile_rbfbias_t_kernel(tc, q, k, v, qs_s, ks_s, alpha, beta, out):
    nc = tc.nc
    with ExitStack() as ctx:
        ctx.enter_context(tc.manual_schedule())
        const = ctx.enter_context(tc.tile_pool(name="const", bufs=1))
        raw = ctx.enter_context(tc.tile_pool(name="raw", bufs=1))
        operand = ctx.enter_context(tc.tile_pool(name="operand", bufs=1))
        work = ctx.enter_context(tc.tile_pool(name="work", bufs=2))
        psum = ctx.enter_context(tc.psum_pool(name="psum", bufs=2))

        def k_due(step):
            h, rest = divmod(step + 11, 2)
            if rest == 0 and 0 <= h < H:
                return (0, h)
            h = due(step, 0, H)
            return None if h is None else (1, h)

        def v_due(step):
            if 0 <= step + 3 < H:
                return (0, step + 3)
            h = due(step, 8, H)
            return None if h is None else (1, h)

        first_step, last_step = -12, UNITS + 6

        ident_bf = const.tile([P, P], BF16)
        make_identity(nc, ident_bf[:])
        ident_f32 = const.tile([P, P], F32)
        make_identity(nc, ident_f32[:])

        pos = const.tile([P, SIDES, POS_PAD], BF16)
        nc.scalar.dma_start(
            out=pos[:, 0, 0 : B * TILES * F].rearrange("p (b x) -> p b x", b=B),
            in_=qs_s.rearrange("b (p t) f -> p b (t f)", t=TILES),
        )
        nc.scalar.dma_start(
            out=pos[:, 1, 0 : B * TILES * F].rearrange("p (x f) -> p x f", f=F),
            in_=ks_s.rearrange("b (t p) f -> p (b t) f", p=P),
        )
        alpha_bf = const.tile([P, H], BF16)
        nc.scalar.dma_start(out=alpha_bf[:], in_=alpha.rearrange("h o -> (h o)").partition_broadcast(P))
        beta_bf = const.tile([P, H], BF16)
        nc.scalar.dma_start(out=beta_bf[:], in_=beta.rearrange("h o -> (h o)").partition_broadcast(P))

        k_raw, q_raw, v_raw, v_grouped = {}, {}, {}, {}
        for s in range(first_step, last_step + 1):
            head = k_due(s)
            if head is not None:
                k_raw[head] = raw.tile([P, TILES, D], BF16, name="k_raw_%d_%d" % head)
                nc.sync.dma_start(out=k_raw[head][:], in_=k[head[0], head[1]].rearrange("(t p) d -> p t d", p=P))
            g = due(s, -12, GROUPS)
            if g is not None:
                q_raw[g] = raw.tile([P, H, D], BF16, name="q_raw_%d" % g)
                nc.sync.dma_start(
                    out=q_raw[g][:], in_=q[g // TILES].rearrange("h (p t) d -> t p h d", t=TILES)[g % TILES]
                )
            head = v_due(s)
            if head is not None:
                v_raw[head] = raw.tile([P, PACK, D], BF16, name="v_raw_%d_%d" % head)
                nc.sync.dma_start(
                    out=v_raw[head][:].rearrange("p (u e) d -> p u (e d)", e=HALVES),
                    in_=v[head[0], head[1]].rearrange("(u p e) d -> p u (e d)", p=P, e=HALVES),
                )
                v_grouped[head] = operand.tile([P, D, PACK], BF16, name="v_grouped_%d_%d" % head, align_bytes=64)
                nc.gpsimd.tensor_scalar(
                    out=v_grouped[head][:],
                    in0=v_raw[head][:].rearrange("p r d -> p d r"),
                    scalar1=1.0,
                    scalar2=0.0,
                    op0=ALU.mult,
                    op1=ALU.add,
                )

        square_at = (F, 3 * F)
        ones_at = (3 * F, F)
        feat = const.tile([P, SIDES, B * TILES, P], BF16)
        nc.vector.memset(feat[:], 0.0)
        for side in range(SIDES):
            nc.vector.memset(feat[:, side, :, ones_at[side] : ones_at[side] + 2 * F], 1.0)
        x = pos[:, :, 0 : B * TILES * F]
        half_square = const.tile([P, SIDES, B * TILES * F], F32)
        nc.vector.scalar_tensor_tensor(out=half_square[:], in0=x, scalar=-0.5, in1=x, op0=ALU.mult, op1=ALU.mult)
        nc.vector.tensor_copy(out=feat[:, :, :, 0:F], in_=x.rearrange("p s (x f) -> p s x f", f=F))
        for part in range(2):
            for side in range(SIDES):
                exact = half_square[:, side, :].rearrange("p (x f) -> p x f", f=F)
                hi = feat[:, side, :, square_at[side] : square_at[side] + F]
                if part == 0:
                    nc.vector.tensor_copy(out=hi, in_=exact)
                else:
                    lo = feat[:, side, :, square_at[side] + F : square_at[side] + 2 * F]
                    nc.vector.tensor_sub(out=lo, in0=exact, in1=hi)
        two_beta = const.tile([P, H], F32)
        nc.vector.tensor_scalar_mul(out=two_beta[:], in0=beta_bf[:], scalar1=2.0)
        alpha_f32 = const.tile([P, H], F32)
        nc.vector.tensor_copy(out=alpha_f32[:], in_=alpha_bf[:])

        k_ps, k_t, q_ps, q_t, v_codes, v_scales = {}, {}, {}, {}, {}, {}
        d_sq, scores, rbf, z, neg_max, row_sum, inv_sum, e_bf = {}, {}, {}, {}, {}, {}, {}, {}
        e_ps, e_grouped, e_codes, e_scales, acc = {}, {}, {}, {}, {}
        feat_ps, feat_t = {}, {}

        def turn_features(b):
            feat_ps[b] = psum.tile([P, SIDES, TILES, P], BF16, tag="acc", name="feat_ps")
            for side in range(SIDES):
                for t in range(TILES):
                    nc.tensor.transpose(feat_ps[b][:, side, t, :], feat[:, side, b * TILES + t, :], ident_bf[:])

        def copy_features(b):
            feat_t[b] = const.tile([P, SIDES, S], BF16, name="feat_t_%d" % b)
            nc.vector.tensor_copy(out=feat_t[b][:].rearrange("f s (t p) -> f s t p", p=P), in_=feat_ps[b][:])

        def turn_k(b, h):
            k_ps[b, h] = psum.tile([P, CHUNKS, S], BF16, tag="turn", name="k_ps")
            for t in range(TILES):
                for c in range(CHUNKS):
                    nc.tensor.transpose(
                        k_ps[b, h][:, c, t * P : (t + 1) * P], k_raw[b, h][:, t, c * P : (c + 1) * P], ident_bf[:]
                    )

        def copy_k(b, h):
            k_t[b, h] = operand.tile([P, CHUNKS, S], BF16, name="k_t_%d_%d" % (b, h))
            nc.scalar.copy(out=k_t[b, h][:], in_=k_ps[b, h][:])

        def turn_q(g):
            q_ps[g] = psum.tile([P, H, CHUNKS, P], BF16, tag="turn", name="q_ps")
            for h in range(H):
                for c in range(CHUNKS):
                    nc.tensor.transpose(q_ps[g][:, h, c, :], q_raw[g][:, h, c * P : (c + 1) * P], ident_bf[:])

        def copy_q(g):
            q_t[g] = work.tile([P, H, CHUNKS, P], BF16, name="q_t", bufs=4)
            nc.vector.tensor_scalar_mul(out=q_t[g][:], in0=q_ps[g][:], scalar1=1.0 / math.sqrt(D))

        def quantise_v(b, h):
            v_codes[b, h] = operand.tile([P, D], U32, name="v_codes_%d_%d" % (b, h), align_bytes=64)
            v_scales[b, h] = operand.tile([P, D], U8, name="v_scales_%d_%d" % (b, h), align_bytes=64)
            nc.vector.quantize_mx(
                out=v_codes[b, h][:].bitcast(FP8X4),
                scales=v_scales[b, h][:],
                in_=v_grouped[b, h][:].rearrange("p d r -> p (d r)"),
            )

        def distances(g):
            b, t = divmod(g, TILES)
            d_sq[g] = psum.tile([P, S], F32, name="d_sq")
            nc.tensor.matmul(
                d_sq[g][:], lhsT=feat_t[b][:, 0, t * P : (t + 1) * P], rhs=feat_t[b][:, 1, :], start=True, stop=True
            )

        def radial(u):
            g, h = divmod(u, H)
            rbf[u] = work.tile([P, S], F32, name="rbf", bufs=6)
            nc.scalar.activation(out=rbf[u][:], in_=d_sq[g][:], func=FUNC.Exp, scale=two_beta[:, h : h + 1])

        def first_matmul(u):
            g, h = divmod(u, H)
            scores[u] = psum.tile([P, S], F32, name="scores")
            for c in range(CHUNKS):
                nc.tensor.matmul(
                    scores[u][:],
                    lhsT=q_t[g][:, h, c, :],
                    rhs=k_t[g // TILES, h][:, c, :],
                    start=(c == 0),
                    stop=(c == CHUNKS - 1),
                )

        def logits(u):
            h = u % H
            z[u] = work.tile([P, S], F32, name="z", bufs=8)
            nc.vector.scalar_tensor_tensor(
                out=z[u][:], in0=rbf[u][:], scalar=alpha_f32[:, h : h + 1], in1=scores[u][:], op0=ALU.mult, op1=ALU.add
            )

        def row_max(u):
            g, h = divmod(u, H)
            if h == 0:
                neg_max[g] = work.tile([P, H], F32, name="neg_max", bufs=3)
            nc.vector.tensor_reduce(out=neg_max[g][:, h : h + 1], in_=z[u][:], axis=AXIS.X, op=ALU.max, negate=True)

        def exponent(u):
            g, h = divmod(u, H)
            if h == 0:
                e_bf[g] = work.tile([P, H * S], BF16, name="e_bf", bufs=3)
                row_sum[g] = work.tile([P, H], F32, name="row_sum", bufs=3)
            nc.scalar.activation(
                out=e_bf[g][:, h * S : (h + 1) * S],
                in_=z[u][:],
                func=FUNC.Exp,
                bias=neg_max[g][:, h : h + 1],
                accum_out=row_sum[g][:, h : h + 1],
            )

        def turn_e(g, pair):
            e_words = e_bf[g][:].bitcast(F32)
            e_ps[g, pair] = psum.tile([P, PAIR, HALVES, P], F32, tag="turn", name="e_ps")
            for hh in range(PAIR):
                for u in range(HALVES):
                    first = ((pair * PAIR + hh) * HALVES + u) * P
                    nc.tensor.transpose(e_ps[g, pair][:, hh, u, :], e_words[:, first : first + P], ident_f32[:])

        def copy_e(g, pair, copy):
            e_grouped[g, pair] = work.tile([P, PAIR * P * PACK], BF16, name="e_grouped", bufs=4, align_bytes=64)
            copy(
                out=e_grouped[g, pair][:].bitcast(F32).rearrange("p (h i u) -> p h i u", h=PAIR, u=HALVES),
                in_=e_ps[g, pair][:].rearrange("p h u i -> p h i u"),
            )

        def quantise_e(g, pair):
            e_codes[g, pair] = work.tile([P, PAIR * P], U32, name="e_codes", bufs=3, align_bytes=64)
            e_scales[g, pair] = work.tile([P, PAIR * P], U8, name="e_scales", bufs=3, align_bytes=64)
            nc.vector.quantize_mx(
                out=e_codes[g, pair][:].bitcast(FP8X4), scales=e_scales[g, pair][:], in_=e_grouped[g, pair][:]
            )

        def reciprocal(g):
            inv_sum[g] = work.tile([P, H], F32, name="inv_sum", bufs=3)
            nc.vector.reciprocal(out=inv_sum[g][:], in_=row_sum[g][:])

        def second_matmul(g, pair):
            acc[g, pair] = psum.tile([P, PAIR, D], F32, name="acc")
            for hh in range(PAIR):
                h = pair * PAIR + hh
                nc.tensor.matmul_mx(
                    out=acc[g, pair][:, hh, :],
                    lhsT=e_codes[g, pair][:, hh * P : (hh + 1) * P].bitcast(FP8X4),
                    lhsT_scale=e_scales[g, pair][:, hh * P : (hh + 1) * P],
                    rhs=v_codes[g // TILES, h][:].bitcast(FP8X4),
                    rhs_scale=v_scales[g // TILES, h][:],
                    start=True,
                    stop=True,
                )

        def normalise(g, pair):
            b, t = divmod(g, TILES)
            heads = slice(pair * PAIR, (pair + 1) * PAIR)
            result = work.tile([P, PAIR, D], F32, bufs=4)
            if pair == 0:
                for hh in range(PAIR):
                    nc.scalar.activation(
                        out=result[:, hh, :], in_=acc[g, pair][:, hh, :], func=FUNC.Copy, scale=inv_sum[g][:, hh : hh + 1]
                    )
            else:
                nc.vector.tensor_tensor(
                    out=result[:],
                    in0=acc[g, pair][:],
                    in1=inv_sum[g][:, heads].unsqueeze(2).to_broadcast([P, PAIR, D]),
                    op=ALU.mult,
                )
            nc.sync.dma_start(out=out[b].rearrange("h (p t) d -> t p h d", t=TILES)[t, :, heads, :], in_=result[:])

        for s in range(first_step, last_step + 1):
            if 0 <= s + 5 < UNITS:
                first_matmul(s + 5)
            for pair in range(H // PAIR):
                g = due(s, 2 + 4 * pair, GROUPS)
                if g is not None:
                    turn_e(g, pair)
            head = k_due(s)
            if head is not None:
                turn_k(head[0], head[1])
            g = due(s, -12, GROUPS)
            if g is not None:
                turn_q(g)
            b = due(s, -10, GROUPS)
            if b is not None and b % TILES == 0:
                turn_features(b // TILES)
            for pair in range(H // PAIR):
                g = due(s, 9, GROUPS)
                if g is not None:
                    second_matmul(g, pair)
            g = due(s, -8, GROUPS)
            if g is not None:
                distances(g)

            if 0 <= s + 7 < UNITS:
                radial(s + 7)
            if 0 <= s < UNITS:
                exponent(s)
            head = k_due(s - 1)
            if head is not None:
                copy_k(head[0], head[1])
            g = due(s, 3, GROUPS)
            if g is not None:
                copy_e(g, 0, nc.scalar.copy)
            g = due(s, 10, GROUPS)
            if g is not None:
                normalise(g, 0)

            if 0 <= s + 4 < UNITS:
                logits(s + 4)
            if 0 <= s + 3 < UNITS:
                row_max(s + 3)
            b = due(s, -9, GROUPS)
            if b is not None and b % TILES == 0:
                copy_features(b // TILES)
            g = due(s, 6, GROUPS)
            if g is not None:
                reciprocal(g)
            for pair in range(H // PAIR):
                g = due(s, 6 + 2 * pair, GROUPS)
                if g is not None:
                    quantise_e(g, pair)
            g = due(s, 7, GROUPS)
            if g is not None:
                copy_e(g, 1, nc.vector.tensor_copy)
            g = due(s, 10, GROUPS)
            if g is not None:
                normalise(g, 1)
            g = due(s, -11, GROUPS)
            if g is not None:
                copy_q(g)
            head = v_due(s - 3)
            if head is not None:
                quantise_v(head[0], head[1])
